import numpy as np
import ml_dtypes

BF16 = ml_dtypes.bfloat16


def bf(x):
    return np.asarray(x, np.float32).astype(BF16)


def f32(x):
    return np.asarray(x, np.float32)


def f64(x):
    return np.asarray(x).astype(np.float64)


def striped(idx):
    return np.tile(idx.reshape(-1, 16).T, (8, 1))


S, D, M, N, DEG = 4096, 128, 512, 2048, 8


def elu(v):
    return np.maximum(v, 0.0) + np.exp(np.minimum(v, 0.0)) - 1.0


def setup_inputs():
    table = bf(np.random.standard_normal((S, D)))
    w = bf(np.random.standard_normal((D, M)) / np.sqrt(D))
    adj_t = bf(np.maximum(np.random.random((N, N)) < DEG / N, np.eye(N)))
    return {"table": table, "w": w, "adj_t": adj_t, "offs": striped(np.random.permutation(S)[:N])}


def reference(table, w, adj_t, offs):
    idx = offs[:16].T.reshape(-1)
    h = f64(w).T @ f64(table)[idx].T
    nb = f64(adj_t)
    return elu((h @ nb) / nb.sum(axis=0, keepdims=True))

@@ -1,0 +1,135 @@
+import concourse.mybir as mybir
+from concourse.masks import make_identity
+
+P = 128
+S, D, M, N = 4096, 128, 512, 2048
+PIECE = 512
+N_PIECES = N // PIECE
+M_BLOCKS = M // P
+T_BLOCKS = N // P
+T_PER_PIECE = PIECE // P
+FLIPS_PER_BANK = 8
+
+FLOPS = 2 * D * M * N + 2 * M * N * N
+
+BF16, F32, U16 = mybir.dt.bfloat16, mybir.dt.float32, mybir.dt.uint16
+ADD, MULT, MAX = mybir.AluOpType.add, mybir.AluOpType.mult, mybir.AluOpType.max
+COPY, EXP = mybir.ActivationFunctionType.Copy, mybir.ActivationFunctionType.Exp
+
+
+def tile_multiheadgraphchannelattention_kernel(tc, table, w, adj_t, offs, out):
+    nc = tc.nc
+    with (
+        tc.tile_pool(name="held", bufs=1) as held,
+        tc.tile_pool(name="work", bufs=3) as work,
+        tc.psum_pool(name="flips", bufs=2) as flips,
+        tc.psum_pool(name="banks", bufs=6) as banks,
+    ):
+        offsets = held.tile([P, N // 16], U16, name="offsets")
+        nc.sync.dma_start(offsets[:], offs)
+        weights = held.tile([D, M], BF16, name="weights")
+        nc.scalar.dma_start(weights[:], w)
+
+        rows = held.tile([P, S // P, D], BF16, name="rows")
+        table_blocks = table.rearrange("(b p) k -> p b k", p=P)
+        n_banks_of_table = S // (P * FLIPS_PER_BANK)
+        for c in range(n_banks_of_table):
+            blocks = slice(c * FLIPS_PER_BANK, (c + 1) * FLIPS_PER_BANK)
+            queue = nc.sync if c % 2 == 0 else nc.scalar
+            queue.dma_start(rows[:, blocks, :], table_blocks[:, blocks, :])
+
+        adj = [held.tile([P, T_BLOCKS, PIECE], BF16, name=f"adj{j}") for j in range(N_PIECES)]
+        adj_blocks = adj_t.rearrange("(b p) j -> p b j", p=P)
+        for j in range(N_PIECES):
+            for b in range(0, T_BLOCKS, T_PER_PIECE):
+                nc.sync.dma_start(
+                    adj[j][:, b : b + T_PER_PIECE, :],
+                    adj_blocks[:, b : b + T_PER_PIECE, j * PIECE : (j + 1) * PIECE],
+                )
+
+        identity = held.tile([P, P], BF16, name="identity")
+        make_identity(nc, identity[:])
+        ones = held.tile([P, P], BF16, name="ones")
+        nc.vector.memset(ones[:], 1.0)
+
+        window = held.tile([D, S], BF16, name="window")
+        for c in range(n_banks_of_table):
+            flipped = flips.tile([P, FLIPS_PER_BANK * P], BF16, name="flipped")
+            for i in range(FLIPS_PER_BANK):
+                nc.tensor.transpose(
+                    flipped[:, i * P : (i + 1) * P], rows[:, c * FLIPS_PER_BANK + i, :], identity[:]
+                )
+            columns = slice(c * FLIPS_PER_BANK * P, (c + 1) * FLIPS_PER_BANK * P)
+            nc.vector.tensor_copy(window[:, columns], flipped[:])
+
+        h = [held.tile([P, M_BLOCKS, PIECE], BF16, name=f"h{c}") for c in range(N_PIECES)]
+        h_t = [held.tile([P, 2, M], BF16, name=f"h_t{i}") for i in range(T_BLOCKS // 2)]
+
+        def project(c):
+            picked = window[:].indirect(offsets[:, c * (PIECE // 16) : (c + 1) * (PIECE // 16)])
+            for mb in range(M_BLOCKS):
+                product = banks.tile([P, PIECE], F32, name="bank")
+                nc.tensor.matmul(
+                    product[:], weights[:, mb * P : (mb + 1) * P], picked, start=True, stop=True
+                )
+                if mb % 2 == 0:
+                    nc.vector.tensor_copy(h[c][:, mb, :], product[:])
+                else:
+                    nc.scalar.activation(h[c][:, mb, :], product[:], COPY)
+
+        def flip(c):
+            for pair in range(T_PER_PIECE // 2):
+                flipped = flips.tile([P, 2, M], BF16, name="flipped")
+                for q in range(2):
+                    t0 = (2 * pair + q) * P
+                    for mb in range(M_BLOCKS):
+                        nc.tensor.transpose(
+                            flipped[:, q, mb * P : (mb + 1) * P], h[c][:, mb, t0 : t0 + P], identity[:]
+                        )
+                nc.vector.tensor_copy(h_t[c * (T_PER_PIECE // 2) + pair][:], flipped[:])
+
+        for c in range(N_PIECES):
+            project(c)
+            if c > 0:
+                flip(c - 1)
+        flip(N_PIECES - 1)
+
+        def one_over_degree(j):
+            sums = work.tile([P, T_BLOCKS // 2, PIECE], BF16, name="sums", bufs=2)
+            half = T_BLOCKS // 2
+            nc.vector.tensor_tensor(sums[:], adj[j][:, 0:half, :], adj[j][:, half : 2 * half, :], ADD)
+            while half > 1:
+                half //= 2
+                nc.vector.tensor_tensor(
+                    sums[:, 0:half, :], sums[:, 0:half, :], sums[:, half : 2 * half, :], ADD
+                )
+            degree = banks.tile([P, PIECE], F32, name="bank")
+            nc.tensor.matmul(degree[:], ones[:], sums[:, 0, :], start=True, stop=True)
+            inverse = held.tile([P, PIECE], F32, name=f"inverse{j}")
+            nc.vector.reciprocal(inverse[:], degree[:])
+            return inverse
+
+        inverse = one_over_degree(0)
+        for j in range(N_PIECES):
+            inverse_next = None
+            for mb in range(M_BLOCKS):
+                total = banks.tile([P, PIECE], F32, name="bank")
+                for b in range(T_BLOCKS):
+                    nc.tensor.matmul(
+                        total[:],
+                        h_t[b // 2][:, b % 2, mb * P : (mb + 1) * P],
+                        adj[j][:, b, :],
+                        start=(b == 0),
+                        stop=(b == T_BLOCKS - 1),
+                    )
+                if mb == 1 and j + 1 < N_PIECES:
+                    inverse_next = one_over_degree(j + 1)
+                mean = work.tile([P, PIECE], F32, name="mean")
+                nc.vector.tensor_tensor(mean[:], total[:], inverse[:], MULT)
+                tail = work.tile([P, PIECE], F32, name="tail")
+                nc.vector.tensor_scalar_min(tail[:], mean[:], 0.0)
+                nc.scalar.activation(tail[:], tail[:], EXP)
+                result = work.tile([P, PIECE], F32, name="result")
+                nc.vector.scalar_tensor_tensor(result[:], tail[:], -1.0, mean[:], ADD, MAX)
+                nc.sync.dma_start(out[mb * P : (mb + 1) * P, j * PIECE : (j + 1) * PIECE], result[:])
+            inverse = inverse_next

@@ -94,7 +94,7 @@ def tile_multiheadgraphchannelattention_kernel(tc, table, w, adj_t, offs, out):
                 flip(c - 1)
         flip(N_PIECES - 1)
 
-        def one_over_degree(j):
+        def column_sums(j):
             sums = work.tile([P, T_BLOCKS // 2, PIECE], BF16, name="sums", bufs=2)
             half = T_BLOCKS // 2
             nc.vector.tensor_tensor(sums[:], adj[j][:, 0:half, :], adj[j][:, half : 2 * half, :], ADD)
@@ -103,33 +103,47 @@ def tile_multiheadgraphchannelattention_kernel(tc, table, w, adj_t, offs, out):
                 nc.vector.tensor_tensor(
                     sums[:, 0:half, :], sums[:, 0:half, :], sums[:, half : 2 * half, :], ADD
                 )
+            return sums
+
+        def one_over_degree(j, sums):
             degree = banks.tile([P, PIECE], F32, name="bank")
             nc.tensor.matmul(degree[:], ones[:], sums[:, 0, :], start=True, stop=True)
             inverse = held.tile([P, PIECE], F32, name=f"inverse{j}")
             nc.vector.reciprocal(inverse[:], degree[:])
             return inverse
 
-        inverse = one_over_degree(0)
+        def aggregate(j, mb):
+            total = banks.tile([P, PIECE], F32, name="bank")
+            for b in range(T_BLOCKS):
+                nc.tensor.matmul(
+                    total[:],
+                    h_t[b // 2][:, b % 2, mb * P : (mb + 1) * P],
+                    adj[j][:, b, :],
+                    start=(b == 0),
+                    stop=(b == T_BLOCKS - 1),
+                )
+            return total
+
+        def finish(j, mb, total, inverse):
+            mean = work.tile([P, PIECE], F32, name="mean")
+            nc.vector.tensor_tensor(mean[:], total[:], inverse[:], MULT)
+            tail = work.tile([P, PIECE], F32, name="tail")
+            nc.vector.tensor_scalar_min(tail[:], mean[:], 0.0)
+            nc.scalar.activation(tail[:], tail[:], EXP)
+            result = work.tile([P, PIECE], F32, name="result")
+            nc.vector.scalar_tensor_tensor(result[:], tail[:], -1.0, mean[:], ADD, MAX)
+            nc.sync.dma_start(out[mb * P : (mb + 1) * P, j * PIECE : (j + 1) * PIECE], result[:])
+
+        sums = column_sums(0)
         for j in range(N_PIECES):
-            inverse_next = None
-            for mb in range(M_BLOCKS):
-                total = banks.tile([P, PIECE], F32, name="bank")
-                for b in range(T_BLOCKS):
-                    nc.tensor.matmul(
-                        total[:],
-                        h_t[b // 2][:, b % 2, mb * P : (mb + 1) * P],
-                        adj[j][:, b, :],
-                        start=(b == 0),
-                        stop=(b == T_BLOCKS - 1),
-                    )
-                if mb == 1 and j + 1 < N_PIECES:
-                    inverse_next = one_over_degree(j + 1)
-                mean = work.tile([P, PIECE], F32, name="mean")
-                nc.vector.tensor_tensor(mean[:], total[:], inverse[:], MULT)
-                tail = work.tile([P, PIECE], F32, name="tail")
-                nc.vector.tensor_scalar_min(tail[:], mean[:], 0.0)
-                nc.scalar.activation(tail[:], tail[:], EXP)
-                result = work.tile([P, PIECE], F32, name="result")
-                nc.vector.scalar_tensor_tensor(result[:], tail[:], -1.0, mean[:], ADD, MAX)
-                nc.sync.dma_start(out[mb * P : (mb + 1) * P, j * PIECE : (j + 1) * PIECE], result[:])
-            inverse = inverse_next
+            total_0 = aggregate(j, 0)
+            total_1 = aggregate(j, 1)
+            inverse = one_over_degree(j, sums)
+            finish(j, 0, total_0, inverse)
+            finish(j, 1, total_1, inverse)
+            total_2 = aggregate(j, 2)
+            finish(j, 2, total_2, inverse)
+            total_3 = aggregate(j, 3)
+            if j + 1 < N_PIECES:
+                sums = column_sums(j + 1)
+            finish(j, 3, total_3, inverse)

@@ -9,6 +9,7 @@ M_BLOCKS = M // P
 T_BLOCKS = N // P
 T_PER_PIECE = PIECE // P
 FLIPS_PER_BANK = 8
+TABLE_LOADS = 8
 
 FLOPS = 2 * D * M * N + 2 * M * N * N
 
@@ -22,21 +23,21 @@ def tile_multiheadgraphchannelattention_kernel(tc, table, w, adj_t, offs, out):
     with (
         tc.tile_pool(name="held", bufs=1) as held,
         tc.tile_pool(name="work", bufs=3) as work,
+        tc.tile_pool(name="staging", bufs=2) as staging,
         tc.psum_pool(name="flips", bufs=2) as flips,
         tc.psum_pool(name="banks", bufs=6) as banks,
     ):
+        rows = held.tile([P, S // P, D], BF16, name="rows")
+        table_blocks = table.rearrange("(b p) k -> p b k", p=P)
+        blocks_per_load = S // (P * TABLE_LOADS)
+        for c in range(TABLE_LOADS):
+            blocks = slice(c * blocks_per_load, (c + 1) * blocks_per_load)
+            queue = nc.sync if c % 2 == 0 else nc.scalar
+            queue.dma_start(rows[:, blocks, :], table_blocks[:, blocks, :])
         offsets = held.tile([P, N // 16], U16, name="offsets")
         nc.sync.dma_start(offsets[:], offs)
         weights = held.tile([D, M], BF16, name="weights")
         nc.scalar.dma_start(weights[:], w)
-
-        rows = held.tile([P, S // P, D], BF16, name="rows")
-        table_blocks = table.rearrange("(b p) k -> p b k", p=P)
-        n_banks_of_table = S // (P * FLIPS_PER_BANK)
-        for c in range(n_banks_of_table):
-            blocks = slice(c * FLIPS_PER_BANK, (c + 1) * FLIPS_PER_BANK)
-            queue = nc.sync if c % 2 == 0 else nc.scalar
-            queue.dma_start(rows[:, blocks, :], table_blocks[:, blocks, :])
 
         adj = [held.tile([P, T_BLOCKS, PIECE], BF16, name=f"adj{j}") for j in range(N_PIECES)]
         adj_blocks = adj_t.rearrange("(b p) j -> p b j", p=P)
@@ -53,6 +54,7 @@ def tile_multiheadgraphchannelattention_kernel(tc, table, w, adj_t, offs, out):
         nc.vector.memset(ones[:], 1.0)
 
         window = held.tile([D, S], BF16, name="window")
+        n_banks_of_table = S // (P * FLIPS_PER_BANK)
         for c in range(n_banks_of_table):
             flipped = flips.tile([P, FLIPS_PER_BANK * P], BF16, name="flipped")
             for i in range(FLIPS_PER_BANK):
@@ -62,10 +64,10 @@ def tile_multiheadgraphchannelattention_kernel(tc, table, w, adj_t, offs, out):
             columns = slice(c * FLIPS_PER_BANK * P, (c + 1) * FLIPS_PER_BANK * P)
             nc.vector.tensor_copy(window[:, columns], flipped[:])
 
-        h = [held.tile([P, M_BLOCKS, PIECE], BF16, name=f"h{c}") for c in range(N_PIECES)]
         h_t = [held.tile([P, 2, M], BF16, name=f"h_t{i}") for i in range(T_BLOCKS // 2)]
 
         def project(c):
+            h_piece = staging.tile([P, M_BLOCKS, PIECE], BF16, name="h_piece", tag="staged")
             picked = window[:].indirect(offsets[:, c * (PIECE // 16) : (c + 1) * (PIECE // 16)])
             for mb in range(M_BLOCKS):
                 product = banks.tile([P, PIECE], F32, name="bank")
@@ -73,77 +75,81 @@ def tile_multiheadgraphchannelattention_kernel(tc, table, w, adj_t, offs, out):
                     product[:], weights[:, mb * P : (mb + 1) * P], picked, start=True, stop=True
                 )
                 if mb % 2 == 0:
-                    nc.vector.tensor_copy(h[c][:, mb, :], product[:])
+                    nc.vector.tensor_copy(h_piece[:, mb, :], product[:])
                 else:
-                    nc.scalar.activation(h[c][:, mb, :], product[:], COPY)
+                    nc.scalar.activation(h_piece[:, mb, :], product[:], COPY)
+            return h_piece
 
-        def flip(c):
+        def flip(c, h_piece):
             for pair in range(T_PER_PIECE // 2):
                 flipped = flips.tile([P, 2, M], BF16, name="flipped")
                 for q in range(2):
                     t0 = (2 * pair + q) * P
                     for mb in range(M_BLOCKS):
                         nc.tensor.transpose(
-                            flipped[:, q, mb * P : (mb + 1) * P], h[c][:, mb, t0 : t0 + P], identity[:]
+                            flipped[:, q, mb * P : (mb + 1) * P], h_piece[:, mb, t0 : t0 + P], identity[:]
                         )
                 nc.vector.tensor_copy(h_t[c * (T_PER_PIECE // 2) + pair][:], flipped[:])
 
+        h_before = None
         for c in range(N_PIECES):
-            project(c)
+            h_piece = project(c)
             if c > 0:
-                flip(c - 1)
-        flip(N_PIECES - 1)
+                flip(c - 1, h_before)
+            h_before = h_piece
+        flip(N_PIECES - 1, h_before)
 
         def column_sums(j):
-            sums = work.tile([P, T_BLOCKS // 2, PIECE], BF16, name="sums", bufs=2)
-            half = T_BLOCKS // 2
-            nc.vector.tensor_tensor(sums[:], adj[j][:, 0:half, :], adj[j][:, half : 2 * half, :], ADD)
-            while half > 1:
-                half //= 2
-                nc.vector.tensor_tensor(
-                    sums[:, 0:half, :], sums[:, 0:half, :], sums[:, half : 2 * half, :], ADD
-                )
+            sums = staging.tile([P, PIECE], BF16, name="sums", tag="staged")
+            nc.vector.tensor_tensor(sums[:], adj[j][:, 0, :], adj[j][:, 1, :], ADD)
+            for b in range(2, T_BLOCKS):
+                nc.vector.tensor_tensor(sums[:], sums[:], adj[j][:, b, :], ADD)
             return sums
 
         def one_over_degree(j, sums):
             degree = banks.tile([P, PIECE], F32, name="bank")
-            nc.tensor.matmul(degree[:], ones[:], sums[:, 0, :], start=True, stop=True)
+            nc.tensor.matmul(degree[:], ones[:], sums[:], start=True, stop=True)
             inverse = held.tile([P, PIECE], F32, name=f"inverse{j}")
             nc.vector.reciprocal(inverse[:], degree[:])
             return inverse
 
-        def aggregate(j, mb):
-            total = banks.tile([P, PIECE], F32, name="bank")
+        def aggregate(j, mb, first, width):
+            total = banks.tile([P, width], F32, name="bank")
             for b in range(T_BLOCKS):
                 nc.tensor.matmul(
                     total[:],
                     h_t[b // 2][:, b % 2, mb * P : (mb + 1) * P],
-                    adj[j][:, b, :],
+                    adj[j][:, b, first : first + width],
                     start=(b == 0),
                     stop=(b == T_BLOCKS - 1),
                 )
             return total
 
-        def finish(j, mb, total, inverse):
-            mean = work.tile([P, PIECE], F32, name="mean")
-            nc.vector.tensor_tensor(mean[:], total[:], inverse[:], MULT)
-            tail = work.tile([P, PIECE], F32, name="tail")
+        def finish(j, mb, first, width, total, inverse):
+            mean = work.tile([P, width], F32, name="mean")
+            nc.vector.tensor_tensor(mean[:], total[:], inverse[:, first : first + width], MULT)
+            tail = work.tile([P, width], F32, name="tail")
             nc.vector.tensor_scalar_min(tail[:], mean[:], 0.0)
             nc.scalar.activation(tail[:], tail[:], EXP)
-            result = work.tile([P, PIECE], F32, name="result")
+            result = work.tile([P, width], F32, name="result")
             nc.vector.scalar_tensor_tensor(result[:], tail[:], -1.0, mean[:], ADD, MAX)
-            nc.sync.dma_start(out[mb * P : (mb + 1) * P, j * PIECE : (j + 1) * PIECE], result[:])
+            column = j * PIECE + first
+            nc.sync.dma_start(out[mb * P : (mb + 1) * P, column : column + width], result[:])
 
         sums = column_sums(0)
         for j in range(N_PIECES):
-            total_0 = aggregate(j, 0)
-            total_1 = aggregate(j, 1)
+            total_0 = aggregate(j, 0, 0, PIECE)
+            total_1 = aggregate(j, 1, 0, PIECE)
             inverse = one_over_degree(j, sums)
-            finish(j, 0, total_0, inverse)
-            finish(j, 1, total_1, inverse)
-            total_2 = aggregate(j, 2)
-            finish(j, 2, total_2, inverse)
-            total_3 = aggregate(j, 3)
+            finish(j, 0, 0, PIECE, total_0, inverse)
+            finish(j, 1, 0, PIECE, total_1, inverse)
+            total_2 = aggregate(j, 2, 0, PIECE)
+            finish(j, 2, 0, PIECE, total_2, inverse)
             if j + 1 < N_PIECES:
+                total_3 = aggregate(j, 3, 0, PIECE)
                 sums = column_sums(j + 1)
-            finish(j, 3, total_3, inverse)
+                finish(j, 3, 0, PIECE, total_3, inverse)
+            else:
+                for first in range(0, PIECE, PIECE // 2):
+                    total_3 = aggregate(j, 3, first, PIECE // 2)
+                    finish(j, 3, first, PIECE // 2, total_3, inverse)

@@ -8,8 +8,8 @@ N_PIECES = N // PIECE
 M_BLOCKS = M // P
 T_BLOCKS = N // P
 T_PER_PIECE = PIECE // P
-FLIPS_PER_BANK = 8
-TABLE_LOADS = 8
+RUN = 4
+WARM_UP = 18
 
 FLOPS = 2 * D * M * N + 2 * M * N * N
 
@@ -24,20 +24,18 @@ def tile_multiheadgraphchannelattention_kernel(tc, table, w, adj_t, offs, out):
         tc.tile_pool(name="held", bufs=1) as held,
         tc.tile_pool(name="work", bufs=3) as work,
         tc.tile_pool(name="staging", bufs=2) as staging,
-        tc.psum_pool(name="flips", bufs=2) as flips,
-        tc.psum_pool(name="banks", bufs=6) as banks,
+        tc.psum_pool(name="banks", bufs=8) as banks,
     ):
-        rows = held.tile([P, S // P, D], BF16, name="rows")
-        table_blocks = table.rearrange("(b p) k -> p b k", p=P)
-        blocks_per_load = S // (P * TABLE_LOADS)
-        for c in range(TABLE_LOADS):
-            blocks = slice(c * blocks_per_load, (c + 1) * blocks_per_load)
-            queue = nc.sync if c % 2 == 0 else nc.scalar
-            queue.dma_start(rows[:, blocks, :], table_blocks[:, blocks, :])
+        n_groups = S // (P * RUN)
+        rows = held.tile([P, n_groups, RUN, D], BF16, name="rows")
+        table_groups = table.rearrange("(g p r) k -> p g r k", p=P, r=RUN)
+        for g in range(n_groups):
+            queue = nc.sync if g % 2 == 0 else nc.scalar
+            queue.dma_start(rows[:, g, :, :], table_groups[:, g, :, :])
         offsets = held.tile([P, N // 16], U16, name="offsets")
         nc.sync.dma_start(offsets[:], offs)
         weights = held.tile([D, M], BF16, name="weights")
-        nc.scalar.dma_start(weights[:], w)
+        nc.sync.dma_start(weights[:], w)
 
         adj = [held.tile([P, T_BLOCKS, PIECE], BF16, name=f"adj{j}") for j in range(N_PIECES)]
         adj_blocks = adj_t.rearrange("(b p) j -> p b j", p=P)
@@ -53,16 +51,21 @@ def tile_multiheadgraphchannelattention_kernel(tc, table, w, adj_t, offs, out):
         ones = held.tile([P, P], BF16, name="ones")
         nc.vector.memset(ones[:], 1.0)
 
+        warm = banks.tile([P, P], F32, name="bank")
+        for i in range(WARM_UP):
+            nc.tensor.matmul(warm[:], ones[:], ones[:], start=True, stop=True)
+
         window = held.tile([D, S], BF16, name="window")
-        n_banks_of_table = S // (P * FLIPS_PER_BANK)
-        for c in range(n_banks_of_table):
-            flipped = flips.tile([P, FLIPS_PER_BANK * P], BF16, name="flipped")
-            for i in range(FLIPS_PER_BANK):
-                nc.tensor.transpose(
-                    flipped[:, i * P : (i + 1) * P], rows[:, c * FLIPS_PER_BANK + i, :], identity[:]
-                )
-            columns = slice(c * FLIPS_PER_BANK * P, (c + 1) * FLIPS_PER_BANK * P)
-            nc.vector.tensor_copy(window[:, columns], flipped[:])
+        for g in range(n_groups):
+            flipped = banks.tile([P, RUN, P], BF16, name="bank")
+            for r in range(RUN):
+                nc.tensor.transpose(flipped[:, r, :], rows[:, g, r, :], identity[:])
+            in_order = flipped[:].rearrange("k r p -> k p r")
+            columns = window[:, g * P * RUN : (g + 1) * P * RUN].rearrange("k (p r) -> k p r", r=RUN)
+            if g % 2 == 0:
+                nc.vector.tensor_copy(columns, in_order)
+            else:
+                nc.scalar.activation(columns, in_order, COPY)
 
         h_t = [held.tile([P, 2, M], BF16, name=f"h_t{i}") for i in range(T_BLOCKS // 2)]
 
@@ -82,7 +85,7 @@ def tile_multiheadgraphchannelattention_kernel(tc, table, w, adj_t, offs, out):
 
         def flip(c, h_piece):
             for pair in range(T_PER_PIECE // 2):
-                flipped = flips.tile([P, 2, M], BF16, name="flipped")
+                flipped = banks.tile([P, 2, M], BF16, name="bank")
                 for q in range(2):
                     t0 = (2 * pair + q) * P
                     for mb in range(M_BLOCKS):

@@ -103,15 +103,19 @@ def tile_multiheadgraphchannelattention_kernel(tc, table, w, adj_t, offs, out):
         flip(N_PIECES - 1, h_before)
 
         def column_sums(j):
-            sums = staging.tile([P, PIECE], BF16, name="sums", tag="staged")
-            nc.vector.tensor_tensor(sums[:], adj[j][:, 0, :], adj[j][:, 1, :], ADD)
-            for b in range(2, T_BLOCKS):
-                nc.vector.tensor_tensor(sums[:], sums[:], adj[j][:, b, :], ADD)
+            sums = staging.tile([P, T_BLOCKS // 2, PIECE], BF16, name="sums", tag="staged")
+            half = T_BLOCKS // 2
+            nc.vector.tensor_tensor(sums[:], adj[j][:, 0:half, :], adj[j][:, half : 2 * half, :], ADD)
+            while half > 1:
+                half //= 2
+                nc.vector.tensor_tensor(
+                    sums[:, 0:half, :], sums[:, 0:half, :], sums[:, half : 2 * half, :], ADD
+                )
             return sums
 
         def one_over_degree(j, sums):
             degree = banks.tile([P, PIECE], F32, name="bank")
-            nc.tensor.matmul(degree[:], ones[:], sums[:], start=True, stop=True)
+            nc.tensor.matmul(degree[:], ones[:], sums[:, 0, :], start=True, stop=True)
             inverse = held.tile([P, PIECE], F32, name=f"inverse{j}")
             nc.vector.reciprocal(inverse[:], degree[:])
             return inverse

@@ -14,7 +14,8 @@ WARM_UP = 18
 FLOPS = 2 * D * M * N + 2 * M * N * N
 
 BF16, F32, U16 = mybir.dt.bfloat16, mybir.dt.float32, mybir.dt.uint16
-ADD, MULT, MAX = mybir.AluOpType.add, mybir.AluOpType.mult, mybir.AluOpType.max
+ADD, MULT = mybir.AluOpType.add, mybir.AluOpType.mult
+MAX, MIN = mybir.AluOpType.max, mybir.AluOpType.min
 COPY, EXP = mybir.ActivationFunctionType.Copy, mybir.ActivationFunctionType.Exp
 
 
@@ -133,11 +134,12 @@ def tile_multiheadgraphchannelattention_kernel(tc, table, w, adj_t, offs, out):
             return total
 
         def finish(j, mb, first, width, total, inverse):
-            mean = work.tile([P, width], F32, name="mean")
-            nc.vector.tensor_tensor(mean[:], total[:], inverse[:, first : first + width], MULT)
+            divisor = inverse[:, first : first + width]
             tail = work.tile([P, width], F32, name="tail")
-            nc.vector.tensor_scalar_min(tail[:], mean[:], 0.0)
+            nc.vector.scalar_tensor_tensor(tail[:], total[:], 0.0, divisor, MIN, MULT)
             nc.scalar.activation(tail[:], tail[:], EXP)
+            mean = work.tile([P, width], F32, name="mean")
+            nc.vector.tensor_tensor(mean[:], total[:], divisor, MULT)
             result = work.tile([P, width], F32, name="result")
             nc.vector.scalar_tensor_tensor(result[:], tail[:], -1.0, mean[:], ADD, MAX)
             column = j * PIECE + first
@@ -145,18 +147,26 @@ def tile_multiheadgraphchannelattention_kernel(tc, table, w, adj_t, offs, out):
 
         sums = column_sums(0)
         for j in range(N_PIECES):
-            total_0 = aggregate(j, 0, 0, PIECE)
-            total_1 = aggregate(j, 1, 0, PIECE)
-            inverse = one_over_degree(j, sums)
-            finish(j, 0, 0, PIECE, total_0, inverse)
+            if j == 0:
+                total_0 = aggregate(j, 0, 0, PIECE)
+                total_1 = aggregate(j, 1, 0, PIECE)
+                inverse = one_over_degree(j, sums)
+                finish(j, 0, 0, PIECE, total_0, inverse)
+            else:
+                total_0 = aggregate(j, 0, 0, PIECE)
+                finish(j, 0, 0, PIECE, total_0, inverse)
+                total_1 = aggregate(j, 1, 0, PIECE)
             finish(j, 1, 0, PIECE, total_1, inverse)
+            if j + 1 < N_PIECES:
+                sums = column_sums(j + 1)
             total_2 = aggregate(j, 2, 0, PIECE)
             finish(j, 2, 0, PIECE, total_2, inverse)
             if j + 1 < N_PIECES:
                 total_3 = aggregate(j, 3, 0, PIECE)
-                sums = column_sums(j + 1)
+                next_inverse = one_over_degree(j + 1, sums)
                 finish(j, 3, 0, PIECE, total_3, inverse)
+                inverse = next_inverse
             else:
-                for first in range(0, PIECE, PIECE // 2):
-                    total_3 = aggregate(j, 3, first, PIECE // 2)
-                    finish(j, 3, first, PIECE // 2, total_3, inverse)
+                for first, width in ((0, PIECE // 2), (PIECE // 2, PIECE // 4), (3 * PIECE // 4, PIECE // 4)):
+                    total_3 = aggregate(j, 3, first, width)
+                    finish(j, 3, first, width, total_3, inverse)

@@ -8,6 +8,7 @@ N_PIECES = N // PIECE
 M_BLOCKS = M // P
 T_BLOCKS = N // P
 T_PER_PIECE = PIECE // P
+SQUARE = 32
 RUN = 4
 WARM_UP = 18
 
@@ -25,6 +26,7 @@ def tile_multiheadgraphchannelattention_kernel(tc, table, w, adj_t, offs, out):
         tc.tile_pool(name="held", bufs=1) as held,
         tc.tile_pool(name="work", bufs=3) as work,
         tc.tile_pool(name="staging", bufs=2) as staging,
+        tc.tile_pool(name="divisors", bufs=2) as divisors,
         tc.psum_pool(name="banks", bufs=8) as banks,
     ):
         n_groups = S // (P * RUN)
@@ -47,10 +49,18 @@ def tile_multiheadgraphchannelattention_kernel(tc, table, w, adj_t, offs, out):
                     adj_blocks[:, b : b + T_PER_PIECE, j * PIECE : (j + 1) * PIECE],
                 )
 
+        ones = held.tile([P, P], BF16, name="ones")
+        nc.gpsimd.memset(ones[:], 1.0)
         identity = held.tile([P, P], BF16, name="identity")
         make_identity(nc, identity[:])
-        ones = held.tile([P, P], BF16, name="ones")
-        nc.vector.memset(ones[:], 1.0)
+
+        quarter = held.tile([P, SQUARE], BF16, name="quarter")
+        with nc.allow_low_precision(reason="a sum of one 1 and three 0s"):
+            nc.vector.tensor_reduce(
+                quarter[:], identity[:].rearrange("k (q i) -> k i q", i=SQUARE), mybir.AxisListType.X, ADD
+            )
+        same_row = held.tile([P, P // SQUARE, SQUARE], BF16, name="same_row")
+        nc.vector.tensor_copy(same_row[:], quarter[:].unsqueeze(1).to_broadcast([P, P // SQUARE, SQUARE]))
 
         warm = banks.tile([P, P], F32, name="bank")
         for i in range(WARM_UP):
@@ -71,7 +81,7 @@ def tile_multiheadgraphchannelattention_kernel(tc, table, w, adj_t, offs, out):
         h_t = [held.tile([P, 2, M], BF16, name=f"h_t{i}") for i in range(T_BLOCKS // 2)]
 
         def project(c):
-            h_piece = staging.tile([P, M_BLOCKS, PIECE], BF16, name="h_piece", tag="staged")
+            h_piece = staging.tile([P, M_BLOCKS, PIECE], BF16, name="h_piece", tag="staged", align_bytes=64)
             picked = window[:].indirect(offsets[:, c * (PIECE // 16) : (c + 1) * (PIECE // 16)])
             for mb in range(M_BLOCKS):
                 product = banks.tile([P, PIECE], F32, name="bank")
@@ -104,7 +114,7 @@ def tile_multiheadgraphchannelattention_kernel(tc, table, w, adj_t, offs, out):
         flip(N_PIECES - 1, h_before)
 
         def column_sums(j):
-            sums = staging.tile([P, T_BLOCKS // 2, PIECE], BF16, name="sums", tag="staged")
+            sums = staging.tile([P, T_BLOCKS // 2, PIECE], BF16, name="sums", tag="staged", align_bytes=64)
             half = T_BLOCKS // 2
             nc.vector.tensor_tensor(sums[:], adj[j][:, 0:half, :], adj[j][:, half : 2 * half, :], ADD)
             while half > 1:
@@ -115,10 +125,29 @@ def tile_multiheadgraphchannelattention_kernel(tc, table, w, adj_t, offs, out):
             return sums
 
         def one_over_degree(j, sums):
-            degree = banks.tile([P, PIECE], F32, name="bank")
-            nc.tensor.matmul(degree[:], ones[:], sums[:, 0, :], start=True, stop=True)
-            inverse = held.tile([P, PIECE], F32, name=f"inverse{j}")
-            nc.vector.reciprocal(inverse[:], degree[:])
+            turned = divisors.tile([P, PIECE], BF16, name="turned", align_bytes=64)
+            nc.vector.transpose(turned[:], sums[:, 0, :])
+            parts = divisors.tile([P, 2, PIECE // SQUARE], BF16, name="parts")
+            with nc.allow_low_precision(reason="whole numbers up to 256"):
+                nc.vector.tensor_reduce(
+                    parts[:].rearrange("p h b -> p b h"),
+                    turned[:].rearrange("p (b h k) -> p b h k", h=2, k=SQUARE // 2),
+                    mybir.AxisListType.X,
+                    ADD,
+                )
+            degree = banks.tile([P, PIECE // SQUARE], F32, name="bank")
+            for h in range(2):
+                nc.tensor.matmul(
+                    degree[:], same_row[:].rearrange("k q i -> k (q i)"), parts[:, h, :], start=(h == 0), stop=(h == 1)
+                )
+            column = divisors.tile([P, PIECE // SQUARE], F32, name="column")
+            nc.vector.reciprocal(column[:], degree[:])
+            spread = divisors.tile([P, PIECE // SQUARE, SQUARE], F32, name="spread", align_bytes=64)
+            nc.scalar.activation(
+                spread[:], column[:].unsqueeze(2).to_broadcast([P, PIECE // SQUARE, SQUARE]), COPY
+            )
+            inverse = held.tile([P, PIECE], F32, name=f"inverse{j}", align_bytes=64)
+            nc.vector.transpose(inverse[:], spread[:].rearrange("p b i -> p (b i)"))
             return inverse
 
         def aggregate(j, mb, first, width):
@@ -146,27 +175,25 @@ def tile_multiheadgraphchannelattention_kernel(tc, table, w, adj_t, offs, out):
             nc.sync.dma_start(out[mb * P : (mb + 1) * P, column : column + width], result[:])
 
         sums = column_sums(0)
-        for j in range(N_PIECES):
-            if j == 0:
-                total_0 = aggregate(j, 0, 0, PIECE)
-                total_1 = aggregate(j, 1, 0, PIECE)
-                inverse = one_over_degree(j, sums)
-                finish(j, 0, 0, PIECE, total_0, inverse)
-            else:
-                total_0 = aggregate(j, 0, 0, PIECE)
-                finish(j, 0, 0, PIECE, total_0, inverse)
-                total_1 = aggregate(j, 1, 0, PIECE)
-            finish(j, 1, 0, PIECE, total_1, inverse)
-            if j + 1 < N_PIECES:
-                sums = column_sums(j + 1)
-            total_2 = aggregate(j, 2, 0, PIECE)
-            finish(j, 2, 0, PIECE, total_2, inverse)
-            if j + 1 < N_PIECES:
-                total_3 = aggregate(j, 3, 0, PIECE)
-                next_inverse = one_over_degree(j + 1, sums)
-                finish(j, 3, 0, PIECE, total_3, inverse)
-                inverse = next_inverse
-            else:
-                for first, width in ((0, PIECE // 2), (PIECE // 2, PIECE // 4), (3 * PIECE // 4, PIECE // 4)):
-                    total_3 = aggregate(j, 3, first, width)
-                    finish(j, 3, first, width, total_3, inverse)
+        totals = [aggregate(0, mb, 0, PIECE) for mb in range(3)]
+        inverse = one_over_degree(0, sums)
+        for mb in range(3):
+            finish(0, mb, 0, PIECE, totals[mb], inverse)
+        sums = column_sums(1)
+        total = aggregate(0, 3, 0, PIECE)
+        next_inverse = one_over_degree(1, sums)
+        finish(0, 3, 0, PIECE, total, inverse)
+        for j in range(1, N_PIECES):
+            inverse = next_inverse
+            for mb in range(M_BLOCKS):
+                if j + 1 == N_PIECES and mb + 1 == M_BLOCKS:
+                    for first, width in ((0, PIECE // 2), (PIECE // 2, PIECE // 4), (3 * PIECE // 4, PIECE // 4)):
+                        total = aggregate(j, mb, first, width)
+                        finish(j, mb, first, width, total, inverse)
+                else:
+                    total = aggregate(j, mb, 0, PIECE)
+                    if mb + 1 == M_BLOCKS:
+                        next_inverse = one_over_degree(j + 1, sums)
+                    finish(j, mb, 0, PIECE, total, inverse)
+                if mb == 1 and j + 1 < N_PIECES:
+                    sums = column_sums(j + 1)

@@ -8,6 +8,7 @@ N_PIECES = N // PIECE
 M_BLOCKS = M // P
 T_BLOCKS = N // P
 T_PER_PIECE = PIECE // P
+LAG = 3
 SQUARE = 32
 RUN = 4
 WARM_UP = 18
@@ -25,7 +26,7 @@ def tile_multiheadgraphchannelattention_kernel(tc, table, w, adj_t, offs, out):
     with (
         tc.tile_pool(name="held", bufs=1) as held,
         tc.tile_pool(name="work", bufs=3) as work,
-        tc.tile_pool(name="staging", bufs=2) as staging,
+        tc.tile_pool(name="staging", bufs=LAG + 1) as staging,
         tc.tile_pool(name="divisors", bufs=2) as divisors,
         tc.psum_pool(name="banks", bufs=8) as banks,
     ):
@@ -78,40 +79,34 @@ def tile_multiheadgraphchannelattention_kernel(tc, table, w, adj_t, offs, out):
             else:
                 nc.scalar.activation(columns, in_order, COPY)
 
-        h_t = [held.tile([P, 2, M], BF16, name=f"h_t{i}") for i in range(T_BLOCKS // 2)]
+        h_t = {}
 
-        def project(c):
-            h_piece = staging.tile([P, M_BLOCKS, PIECE], BF16, name="h_piece", tag="staged", align_bytes=64)
+        def project(c, mb):
             picked = window[:].indirect(offsets[:, c * (PIECE // 16) : (c + 1) * (PIECE // 16)])
-            for mb in range(M_BLOCKS):
-                product = banks.tile([P, PIECE], F32, name="bank")
-                nc.tensor.matmul(
-                    product[:], weights[:, mb * P : (mb + 1) * P], picked, start=True, stop=True
-                )
-                if mb % 2 == 0:
-                    nc.vector.tensor_copy(h_piece[:, mb, :], product[:])
-                else:
-                    nc.scalar.activation(h_piece[:, mb, :], product[:], COPY)
-            return h_piece
+            product = banks.tile([P, PIECE], F32, name="bank")
+            nc.tensor.matmul(product[:], weights[:, mb * P : (mb + 1) * P], picked, start=True, stop=True)
+            h = staging.tile([P, PIECE], BF16, name="h", tag="staged", align_bytes=64)
+            if mb % 2 == 0:
+                nc.vector.tensor_copy(h[:], product[:])
+            else:
+                nc.scalar.activation(h[:], product[:], COPY)
+            return h
 
-        def flip(c, h_piece):
-            for pair in range(T_PER_PIECE // 2):
-                flipped = banks.tile([P, 2, M], BF16, name="bank")
-                for q in range(2):
-                    t0 = (2 * pair + q) * P
-                    for mb in range(M_BLOCKS):
-                        nc.tensor.transpose(
-                            flipped[:, q, mb * P : (mb + 1) * P], h_piece[:, mb, t0 : t0 + P], identity[:]
-                        )
-                nc.vector.tensor_copy(h_t[c * (T_PER_PIECE // 2) + pair][:], flipped[:])
+        def flip(c, mb, h):
+            flipped = banks.tile([P, T_PER_PIECE, P], BF16, name="bank")
+            for b in range(T_PER_PIECE):
+                nc.tensor.transpose(flipped[:, b, :], h[:, b * P : (b + 1) * P], identity[:])
+            h_t[c, mb] = held.tile([P, T_PER_PIECE, P], BF16, name=f"h_t{c}_{mb}")
+            nc.vector.tensor_copy(h_t[c, mb][:], flipped[:])
 
-        h_before = None
-        for c in range(N_PIECES):
-            h_piece = project(c)
-            if c > 0:
-                flip(c - 1, h_before)
-            h_before = h_piece
-        flip(N_PIECES - 1, h_before)
+        units = [(c, mb) for c in range(N_PIECES) for mb in range(M_BLOCKS)]
+        h = {}
+        for u, (c, mb) in enumerate(units):
+            h[c, mb] = project(c, mb)
+            if u >= LAG:
+                flip(*units[u - LAG], h[units[u - LAG]])
+        for c, mb in units[len(units) - LAG :]:
+            flip(c, mb, h[c, mb])
 
         def column_sums(j):
             sums = staging.tile([P, T_BLOCKS // 2, PIECE], BF16, name="sums", tag="staged", align_bytes=64)
@@ -155,7 +150,7 @@ def tile_multiheadgraphchannelattention_kernel(tc, table, w, adj_t, offs, out):
             for b in range(T_BLOCKS):
                 nc.tensor.matmul(
                     total[:],
-                    h_t[b // 2][:, b % 2, mb * P : (mb + 1) * P],
+                    h_t[b // T_PER_PIECE, mb][:, b % T_PER_PIECE, :],
                     adj[j][:, b, first : first + width],
                     start=(b == 0),
                     stop=(b == T_BLOCKS - 1),

@@ -105,8 +105,6 @@ def tile_multiheadgraphchannelattention_kernel(tc, table, w, adj_t, offs, out):
             h[c, mb] = project(c, mb)
             if u >= LAG:
                 flip(*units[u - LAG], h[units[u - LAG]])
-        for c, mb in units[len(units) - LAG :]:
-            flip(c, mb, h[c, mb])
 
         def column_sums(j):
             sums = staging.tile([P, T_BLOCKS // 2, PIECE], BF16, name="sums", tag="staged", align_bytes=64)
@@ -170,7 +168,10 @@ def tile_multiheadgraphchannelattention_kernel(tc, table, w, adj_t, offs, out):
             nc.sync.dma_start(out[mb * P : (mb + 1) * P, column : column + width], result[:])
 
         sums = column_sums(0)
-        totals = [aggregate(0, mb, 0, PIECE) for mb in range(3)]
+        totals = [aggregate(0, 0, 0, PIECE)]
+        for c, mb in units[len(units) - LAG :]:
+            flip(c, mb, h[c, mb])
+        totals.extend([aggregate(0, mb, 0, PIECE) for mb in range(1, 3)])
         inverse = one_over_degree(0, sums)
         for mb in range(3):
             finish(0, mb, 0, PIECE, totals[mb], inverse)

import concourse.mybir as mybir
from concourse.masks import make_identity

P = 128
S, D, M, N = 4096, 128, 512, 2048
PIECE = 512
N_PIECES = N // PIECE
M_BLOCKS = M // P
T_BLOCKS = N // P
T_PER_PIECE = PIECE // P
LAG = 3
SQUARE = 32
RUN = 4
WARM_UP = 18

FLOPS = 2 * D * M * N + 2 * M * N * N

BF16, F32, U16 = mybir.dt.bfloat16, mybir.dt.float32, mybir.dt.uint16
ADD, MULT = mybir.AluOpType.add, mybir.AluOpType.mult
MAX, MIN = mybir.AluOpType.max, mybir.AluOpType.min
COPY, EXP = mybir.ActivationFunctionType.Copy, mybir.ActivationFunctionType.Exp


def tile_multiheadgraphchannelattention_kernel(tc, table, w, adj_t, offs, out):
    nc = tc.nc
    with (
        tc.tile_pool(name="held", bufs=1) as held,
        tc.tile_pool(name="work", bufs=3) as work,
        tc.tile_pool(name="staging", bufs=LAG + 1) as staging,
        tc.tile_pool(name="divisors", bufs=2) as divisors,
        tc.psum_pool(name="banks", bufs=8) as banks,
    ):
        n_groups = S // (P * RUN)
        rows = held.tile([P, n_groups, RUN, D], BF16, name="rows")
        table_groups = table.rearrange("(g p r) k -> p g r k", p=P, r=RUN)
        for g in range(n_groups):
            queue = nc.sync if g % 2 == 0 else nc.scalar
            queue.dma_start(rows[:, g, :, :], table_groups[:, g, :, :])
        offsets = held.tile([P, N // 16], U16, name="offsets")
        nc.sync.dma_start(offsets[:], offs)
        weights = held.tile([D, M], BF16, name="weights")
        nc.sync.dma_start(weights[:], w)

        adj = [held.tile([P, T_BLOCKS, PIECE], BF16, name=f"adj{j}") for j in range(N_PIECES)]
        adj_blocks = adj_t.rearrange("(b p) j -> p b j", p=P)
        for j in range(N_PIECES):
            for b in range(0, T_BLOCKS, T_PER_PIECE):
                nc.sync.dma_start(
                    adj[j][:, b : b + T_PER_PIECE, :],
                    adj_blocks[:, b : b + T_PER_PIECE, j * PIECE : (j + 1) * PIECE],
                )

        ones = held.tile([P, P], BF16, name="ones")
        nc.gpsimd.memset(ones[:], 1.0)
        identity = held.tile([P, P], BF16, name="identity")
        make_identity(nc, identity[:])

        quarter = held.tile([P, SQUARE], BF16, name="quarter")
        with nc.allow_low_precision(reason="a sum of one 1 and three 0s"):
            nc.vector.tensor_reduce(
                quarter[:], identity[:].rearrange("k (q i) -> k i q", i=SQUARE), mybir.AxisListType.X, ADD
            )
        same_row = held.tile([P, P // SQUARE, SQUARE], BF16, name="same_row")
        nc.vector.tensor_copy(same_row[:], quarter[:].unsqueeze(1).to_broadcast([P, P // SQUARE, SQUARE]))

        warm = banks.tile([P, P], F32, name="bank")
        for i in range(WARM_UP):
            nc.tensor.matmul(warm[:], ones[:], ones[:], start=True, stop=True)

        window = held.tile([D, S], BF16, name="window")
        for g in range(n_groups):
            flipped = banks.tile([P, RUN, P], BF16, name="bank")
            for r in range(RUN):
                nc.tensor.transpose(flipped[:, r, :], rows[:, g, r, :], identity[:])
            in_order = flipped[:].rearrange("k r p -> k p r")
            columns = window[:, g * P * RUN : (g + 1) * P * RUN].rearrange("k (p r) -> k p r", r=RUN)
            if g % 2 == 0:
                nc.vector.tensor_copy(columns, in_order)
            else:
                nc.scalar.activation(columns, in_order, COPY)

        h_t = {}

        def project(c, mb):
            picked = window[:].indirect(offsets[:, c * (PIECE // 16) : (c + 1) * (PIECE // 16)])
            product = banks.tile([P, PIECE], F32, name="bank")
            nc.tensor.matmul(product[:], weights[:, mb * P : (mb + 1) * P], picked, start=True, stop=True)
            h = staging.tile([P, PIECE], BF16, name="h", tag="staged", align_bytes=64)
            if mb % 2 == 0:
                nc.vector.tensor_copy(h[:], product[:])
            else:
                nc.scalar.activation(h[:], product[:], COPY)
            return h

        def flip(c, mb, h):
            flipped = banks.tile([P, T_PER_PIECE, P], BF16, name="bank")
            for b in range(T_PER_PIECE):
                nc.tensor.transpose(flipped[:, b, :], h[:, b * P : (b + 1) * P], identity[:])
            h_t[c, mb] = held.tile([P, T_PER_PIECE, P], BF16, name=f"h_t{c}_{mb}")
            nc.vector.tensor_copy(h_t[c, mb][:], flipped[:])

        units = [(c, mb) for c in range(N_PIECES) for mb in range(M_BLOCKS)]
        h = {}
        for u, (c, mb) in enumerate(units):
            h[c, mb] = project(c, mb)
            if u >= LAG:
                flip(*units[u - LAG], h[units[u - LAG]])

        def column_sums(j):
            sums = staging.tile([P, T_BLOCKS // 2, PIECE], BF16, name="sums", tag="staged", align_bytes=64)
            half = T_BLOCKS // 2
            nc.vector.tensor_tensor(sums[:], adj[j][:, 0:half, :], adj[j][:, half : 2 * half, :], ADD)
            while half > 1:
                half //= 2
                nc.vector.tensor_tensor(
                    sums[:, 0:half, :], sums[:, 0:half, :], sums[:, half : 2 * half, :], ADD
                )
            return sums

        def one_over_degree(j, sums):
            turned = divisors.tile([P, PIECE], BF16, name="turned", align_bytes=64)
            nc.vector.transpose(turned[:], sums[:, 0, :])
            parts = divisors.tile([P, 2, PIECE // SQUARE], BF16, name="parts")
            with nc.allow_low_precision(reason="whole numbers up to 256"):
                nc.vector.tensor_reduce(
                    parts[:].rearrange("p h b -> p b h"),
                    turned[:].rearrange("p (b h k) -> p b h k", h=2, k=SQUARE // 2),
                    mybir.AxisListType.X,
                    ADD,
                )
            degree = banks.tile([P, PIECE // SQUARE], F32, name="bank")
            for h in range(2):
                nc.tensor.matmul(
                    degree[:], same_row[:].rearrange("k q i -> k (q i)"), parts[:, h, :], start=(h == 0), stop=(h == 1)
                )
            column = divisors.tile([P, PIECE // SQUARE], F32, name="column")
            nc.vector.reciprocal(column[:], degree[:])
            spread = divisors.tile([P, PIECE // SQUARE, SQUARE], F32, name="spread", align_bytes=64)
            nc.scalar.activation(
                spread[:], column[:].unsqueeze(2).to_broadcast([P, PIECE // SQUARE, SQUARE]), COPY
            )
            inverse = held.tile([P, PIECE], F32, name=f"inverse{j}", align_bytes=64)
            nc.vector.transpose(inverse[:], spread[:].rearrange("p b i -> p (b i)"))
            return inverse

        def aggregate(j, mb, first, width):
            total = banks.tile([P, width], F32, name="bank")
            for b in range(T_BLOCKS):
                nc.tensor.matmul(
                    total[:],
                    h_t[b // T_PER_PIECE, mb][:, b % T_PER_PIECE, :],
                    adj[j][:, b, first : first + width],
                    start=(b == 0),
                    stop=(b == T_BLOCKS - 1),
                )
            return total

        def finish(j, mb, first, width, total, inverse):
            divisor = inverse[:, first : first + width]
            tail = work.tile([P, width], F32, name="tail")
            nc.vector.scalar_tensor_tensor(tail[:], total[:], 0.0, divisor, MIN, MULT)
            nc.scalar.activation(tail[:], tail[:], EXP)
            mean = work.tile([P, width], F32, name="mean")
            nc.vector.tensor_tensor(mean[:], total[:], divisor, MULT)
            result = work.tile([P, width], F32, name="result")
            nc.vector.scalar_tensor_tensor(result[:], tail[:], -1.0, mean[:], ADD, MAX)
            column = j * PIECE + first
            nc.sync.dma_start(out[mb * P : (mb + 1) * P, column : column + width], result[:])

        sums = column_sums(0)
        totals = [aggregate(0, 0, 0, PIECE)]
        for c, mb in units[len(units) - LAG :]:
            flip(c, mb, h[c, mb])
        totals.extend([aggregate(0, mb, 0, PIECE) for mb in range(1, 3)])
        inverse = one_over_degree(0, sums)
        for mb in range(3):
            finish(0, mb, 0, PIECE, totals[mb], inverse)
        sums = column_sums(1)
        total = aggregate(0, 3, 0, PIECE)
        next_inverse = one_over_degree(1, sums)
        finish(0, 3, 0, PIECE, total, inverse)
        for j in range(1, N_PIECES):
            inverse = next_inverse
            for mb in range(M_BLOCKS):
                if j + 1 == N_PIECES and mb + 1 == M_BLOCKS:
                    for first, width in ((0, PIECE // 2), (PIECE // 2, PIECE // 4), (3 * PIECE // 4, PIECE // 4)):
                        total = aggregate(j, mb, first, width)
                        finish(j, mb, first, width, total, inverse)
                else:
                    total = aggregate(j, mb, 0, PIECE)
                    if mb + 1 == M_BLOCKS:
                        next_inverse = one_over_degree(j + 1, sums)
                    finish(j, mb, 0, PIECE, total, inverse)
                if mb == 1 and j + 1 < N_PIECES:
                    sums = column_sums(j + 1)
